import numpy as np
import ml_dtypes


def mxq(x, axis, fmt="e4m3"):
    dtype, down = {"e4m3": (ml_dtypes.float8_e4m3fn, 7), "e5m2": (ml_dtypes.float8_e5m2, 14)}[fmt]
    v = np.moveaxis(np.asarray(x, np.float32).astype(ml_dtypes.bfloat16).astype(np.float64), axis, -1)
    blocks = v.reshape(v.shape[:-1] + (-1, 32))
    amax = np.abs(blocks).max(-1, keepdims=True)
    byte = np.maximum(np.where(amax > 0, np.frexp(amax)[1] - 1 + 127, 0) - down, 1)
    scale = np.exp2(byte - 127.0)
    codes = (blocks / scale).astype(np.float32).astype(dtype).astype(np.float64)
    return np.moveaxis((codes * scale).reshape(v.shape), -1, axis)


WIDE = False


def mx_kscale(k):
    if not WIDE:
        return np.ones(k)
    levels = np.array([10, -10, 5, -5, 0])
    a = np.random.permutation(np.resize(levels, k // 512 * 4)).reshape(k // 512, 4)
    idx = np.arange(k)
    return np.exp2(a[idx // 512, idx % 128 // 32])


BF16 = ml_dtypes.bfloat16


def bf(x):
    return np.asarray(x, np.float32).astype(BF16)


def f64(x):
    return np.asarray(x).astype(np.float64)


M, K, N = 1024, 1024, 128


def binarize(v):
    clipped = np.clip(v, -1.0, 1.0)
    rounded = np.sign(clipped)
    return clipped + (rounded - clipped)


def setup_inputs():
    s = mx_kscale(K)
    keep = (s <= s.min() * 4.0).astype(np.float64)
    return {"x": bf(np.random.standard_normal((M, K)) * (s / s.min())[None, :]),
            "w": bf(np.random.standard_normal((K, N)) / np.sqrt(K) * keep[:, None]),
            "gamma": bf(-(1.0 + 0.1 * np.random.standard_normal(1)) / np.sqrt(keep.sum()))}


def reference(x, w, gamma):
    clamped_w = np.abs(f64(gamma)) * binarize(f64(w))
    return mxq(f64(x), 1, "e4m3") @ mxq(clamped_w, 0, "e4m3")

@@ -1,0 +1,134 @@
+from contextlib import ExitStack
+
+import concourse.mybir as mybir
+from concourse.masks import make_identity
+
+BF16 = mybir.dt.bfloat16
+F32 = mybir.dt.float32
+U32 = mybir.dt.uint32
+U8 = mybir.dt.uint8
+FP8X4 = mybir.dt.float8_e4m3fn_x4
+ACT = mybir.ActivationFunctionType
+ALU = mybir.AluOpType
+
+M, K, N = 1024, 1024, 128
+FLOPS = 2 * M * K * N
+
+P = 128
+PACK = 4
+K_PASS = P * PACK
+PASSES = K // K_PASS
+PAIR = 2
+HALVES = PACK // PAIR
+M_TILES = M // P
+ROUND = 2
+ROUNDS = M_TILES // ROUND
+
+
+def tile_binary_dense_s_kernel(tc, x, w, gamma, out):
+    nc = tc.nc
+    with ExitStack() as ctx:
+        ctx.enter_context(tc.manual_schedule())
+        const = ctx.enter_context(tc.tile_pool(name="const", bufs=1))
+        resident = ctx.enter_context(tc.tile_pool(name="resident", bufs=M_TILES))
+        results = ctx.enter_context(tc.tile_pool(name="results", bufs=ROUNDS))
+        flipped = ctx.enter_context(tc.psum_pool(name="flipped", bufs=2 * ROUND))
+        sums = ctx.enter_context(tc.psum_pool(name="sums", bufs=ROUNDS))
+
+        x_view = x.rearrange("(p j) k -> p j k", j=M_TILES)
+        out_view = out.rearrange("(p j) n -> p j n", j=M_TILES)
+
+        gamma_bf = const.tile([P, 1], BF16)
+        nc.scalar.dma_start(out=gamma_bf[:], in_=gamma.partition_broadcast(P))
+
+        w_raw = const.tile([P, PASSES * HALVES, PAIR, N], BF16)
+        nc.sync.dma_start(
+            out=w_raw[:],
+            in_=w.rearrange("(c p e) n -> p c e n", c=PASSES * HALVES, e=PAIR),
+        )
+
+        x_rows = []
+        for j in range(M_TILES):
+            x_tile = resident.tile([P, K], BF16, name="x_tile")
+            nc.sync.dma_start(out=x_tile[:], in_=x_view[:, j, :])
+            x_rows.append(x_tile)
+
+        ident = const.tile([P, P], F32)
+        make_identity(nc, ident[:])
+
+        gamma_abs = const.tile([P, 1], F32)
+        nc.scalar.activation(out=gamma_abs[:], in_=gamma_bf[:], func=ACT.Abs)
+        w_sign = const.tile([P, PASSES, PACK, N], BF16)
+        nc.scalar.activation(
+            out=w_sign[:].rearrange("p g t n -> p (g t n)"),
+            in_=w_raw[:].rearrange("p c e n -> p (c e n)"),
+            func=ACT.Sign,
+        )
+        wb = const.tile([P, PASSES, N, PACK], BF16, align_bytes=64)
+        nc.vector.tensor_scalar(
+            out=wb[:],
+            in0=w_sign[:].rearrange("p g t n -> p g n t"),
+            scalar1=gamma_abs[:, 0:1],
+            scalar2=None,
+            op0=ALU.mult,
+        )
+        w_codes = const.tile([P, PASSES, N], U32, align_bytes=64)
+        w_scales = const.tile([P, PASSES, N], U8, align_bytes=64)
+        nc.vector.quantize_mx(
+            out=w_codes[:].rearrange("p g n -> p (g n)").bitcast(FP8X4),
+            scales=w_scales[:].rearrange("p g n -> p (g n)"),
+            in_=wb[:].rearrange("p g n t -> p (g n t)"),
+        )
+
+        x_codes = []
+        x_scales = []
+
+        def transpose_round(r):
+            grouped_tiles = []
+            for j in range(ROUND * r, ROUND * (r + 1)):
+                words = x_rows[j][:].bitcast(F32)
+                xt = flipped.tile([P, PASSES * HALVES, P], F32, name="xt")
+                for c in range(PASSES * HALVES):
+                    nc.tensor.transpose(xt[:, c, :], words[:, P * c : P * (c + 1)], ident[:])
+                grouped = resident.tile([P, PASSES * P * PACK], BF16, name="grouped", align_bytes=64)
+                dst = grouped[:].bitcast(F32).rearrange("p (g m u) -> p g m u", g=PASSES, u=HALVES)
+                src = xt[:].rearrange("p (g u) m -> p g m u", u=HALVES)
+                if j % 2 == 0:
+                    nc.scalar.copy(out=dst, in_=src)
+                else:
+                    nc.vector.tensor_copy(out=dst, in_=src)
+                grouped_tiles.append(grouped)
+            for grouped in grouped_tiles:
+                codes = resident.tile([P, PASSES, P], U32, name="codes", align_bytes=64)
+                scales = resident.tile([P, PASSES, P], U8, name="scales", align_bytes=64)
+                nc.vector.quantize_mx(
+                    out=codes[:].rearrange("p g m -> p (g m)").bitcast(FP8X4),
+                    scales=scales[:].rearrange("p g m -> p (g m)"),
+                    in_=grouped[:],
+                )
+                x_codes.append(codes)
+                x_scales.append(scales)
+
+        def multiply_round(r):
+            acc = sums.tile([P, ROUND, N], F32, name="acc")
+            for i in range(ROUND):
+                j = ROUND * r + i
+                for g in range(PASSES):
+                    nc.tensor.matmul_mx(
+                        out=acc[:, i, :],
+                        lhsT=x_codes[j][:, g, :].bitcast(FP8X4),
+                        lhsT_scale=x_scales[j][:, g, :],
+                        rhs=w_codes[:, g, :].bitcast(FP8X4),
+                        rhs_scale=w_scales[:, g, :],
+                        start=(g == 0),
+                        stop=(g == PASSES - 1),
+                    )
+            result = results.tile([P, ROUND, N], F32, name="result")
+            nc.scalar.copy(out=result[:], in_=acc[:])
+            nc.sync.dma_start(out=out_view[:, ROUND * r : ROUND * (r + 1), :], in_=result[:])
+
+        transpose_round(0)
+        for r in range(1, ROUNDS):
+            transpose_round(r)
+            multiply_round(r - 1)
+        multiply_round(ROUNDS - 1)

@@ -23,6 +23,9 @@ HALVES = PACK // PAIR
 M_TILES = M // P
 ROUND = 2
 ROUNDS = M_TILES // ROUND
+LAG = ROUNDS
+W_ROUND = 2
+VECTOR_EVERY = 4
 
 
 def tile_binary_dense_s_kernel(tc, x, w, gamma, out):
@@ -41,14 +44,14 @@ def tile_binary_dense_s_kernel(tc, x, w, gamma, out):
         gamma_bf = const.tile([P, 1], BF16)
         nc.scalar.dma_start(out=gamma_bf[:], in_=gamma.partition_broadcast(P))
 
-        w_raw = const.tile([P, PASSES * HALVES, PAIR, N], BF16)
-        nc.sync.dma_start(
-            out=w_raw[:],
-            in_=w.rearrange("(c p e) n -> p c e n", c=PASSES * HALVES, e=PAIR),
-        )
-
+        w_raw = const.tile([P, PASSES, PACK, N], BF16)
         x_rows = []
         for j in range(M_TILES):
+            if j == ROUND * W_ROUND:
+                nc.sync.dma_start(
+                    out=w_raw[:].rearrange("p g (u e) n -> p (g u) e n", e=PAIR),
+                    in_=w.rearrange("(c p e) n -> p c e n", c=PASSES * HALVES, e=PAIR),
+                )
             x_tile = resident.tile([P, K], BF16, name="x_tile")
             nc.sync.dma_start(out=x_tile[:], in_=x_view[:, j, :])
             x_rows.append(x_tile)
@@ -56,29 +59,31 @@ def tile_binary_dense_s_kernel(tc, x, w, gamma, out):
         ident = const.tile([P, P], F32)
         make_identity(nc, ident[:])
 
-        gamma_abs = const.tile([P, 1], F32)
-        nc.scalar.activation(out=gamma_abs[:], in_=gamma_bf[:], func=ACT.Abs)
-        w_sign = const.tile([P, PASSES, PACK, N], BF16)
-        nc.scalar.activation(
-            out=w_sign[:].rearrange("p g t n -> p (g t n)"),
-            in_=w_raw[:].rearrange("p c e n -> p (c e n)"),
-            func=ACT.Sign,
-        )
-        wb = const.tile([P, PASSES, N, PACK], BF16, align_bytes=64)
-        nc.vector.tensor_scalar(
-            out=wb[:],
-            in0=w_sign[:].rearrange("p g t n -> p g n t"),
-            scalar1=gamma_abs[:, 0:1],
-            scalar2=None,
-            op0=ALU.mult,
-        )
         w_codes = const.tile([P, PASSES, N], U32, align_bytes=64)
         w_scales = const.tile([P, PASSES, N], U8, align_bytes=64)
-        nc.vector.quantize_mx(
-            out=w_codes[:].rearrange("p g n -> p (g n)").bitcast(FP8X4),
-            scales=w_scales[:].rearrange("p g n -> p (g n)"),
-            in_=wb[:].rearrange("p g n t -> p (g n t)"),
-        )
+
+        def prepare_weights():
+            gamma_abs = const.tile([P, 1], F32)
+            nc.scalar.activation(out=gamma_abs[:], in_=gamma_bf[:], func=ACT.Abs)
+            w_sign = const.tile([P, PASSES, N, PACK], BF16)
+            nc.scalar.activation(
+                out=w_sign[:],
+                in_=w_raw[:].rearrange("p g t n -> p g n t"),
+                func=ACT.Sign,
+            )
+            wb = const.tile([P, PASSES * N * PACK], BF16, align_bytes=64)
+            nc.vector.tensor_scalar(
+                out=wb[:],
+                in0=w_sign[:].rearrange("p g n t -> p (g n t)"),
+                scalar1=gamma_abs[:, 0:1],
+                scalar2=None,
+                op0=ALU.mult,
+            )
+            nc.vector.quantize_mx(
+                out=w_codes[:].rearrange("p g n -> p (g n)").bitcast(FP8X4),
+                scales=w_scales[:].rearrange("p g n -> p (g n)"),
+                in_=wb[:],
+            )
 
         x_codes = []
         x_scales = []
@@ -93,10 +98,10 @@ def tile_binary_dense_s_kernel(tc, x, w, gamma, out):
                 grouped = resident.tile([P, PASSES * P * PACK], BF16, name="grouped", align_bytes=64)
                 dst = grouped[:].bitcast(F32).rearrange("p (g m u) -> p g m u", g=PASSES, u=HALVES)
                 src = xt[:].rearrange("p (g u) m -> p g m u", u=HALVES)
-                if j % 2 == 0:
-                    nc.scalar.copy(out=dst, in_=src)
-                else:
+                if j % VECTOR_EVERY == VECTOR_EVERY - 1:
                     nc.vector.tensor_copy(out=dst, in_=src)
+                else:
+                    nc.scalar.copy(out=dst, in_=src)
                 grouped_tiles.append(grouped)
             for grouped in grouped_tiles:
                 codes = resident.tile([P, PASSES, P], U32, name="codes", align_bytes=64)
@@ -127,8 +132,10 @@ def tile_binary_dense_s_kernel(tc, x, w, gamma, out):
             nc.scalar.copy(out=result[:], in_=acc[:])
             nc.sync.dma_start(out=out_view[:, ROUND * r : ROUND * (r + 1), :], in_=result[:])
 
-        transpose_round(0)
-        for r in range(1, ROUNDS):
-            transpose_round(r)
-            multiply_round(r - 1)
-        multiply_round(ROUNDS - 1)
+        for r in range(ROUNDS + LAG):
+            if r == W_ROUND:
+                prepare_weights()
+            if r < ROUNDS:
+                transpose_round(r)
+            if r >= LAG:
+                multiply_round(r - LAG)

@@ -7,6 +7,7 @@ BF16 = mybir.dt.bfloat16
 F32 = mybir.dt.float32
 U32 = mybir.dt.uint32
 U8 = mybir.dt.uint8
+I32 = mybir.dt.int32
 FP8X4 = mybir.dt.float8_e4m3fn_x4
 ACT = mybir.ActivationFunctionType
 ALU = mybir.AluOpType
@@ -23,9 +24,11 @@ HALVES = PACK // PAIR
 M_TILES = M // P
 ROUND = 2
 ROUNDS = M_TILES // ROUND
-LAG = ROUNDS
-W_ROUND = 2
-VECTOR_EVERY = 4
+LAG = 1
+W_ROUND = 0
+VECTOR_EVERY = 3
+WARM_PASSES = 8
+N_WARM = 512
 
 
 def tile_binary_dense_s_kernel(tc, x, w, gamma, out):
@@ -58,6 +61,23 @@ def tile_binary_dense_s_kernel(tc, x, w, gamma, out):
 
         ident = const.tile([P, P], F32)
         make_identity(nc, ident[:])
+
+        zeros = const.tile([P, N_WARM * PACK], BF16, align_bytes=64)
+        zero_codes = const.tile([P, N_WARM], U32, align_bytes=64)
+        zero_scales = const.tile([P, N_WARM], U8, align_bytes=64)
+        nc.vector.memset(zeros[:].bitcast(I32), 0)
+        nc.vector.quantize_mx(out=zero_codes[:].bitcast(FP8X4), scales=zero_scales[:], in_=zeros[:])
+        unread = flipped.tile([P, N_WARM], F32, name="xt")
+        for i in range(WARM_PASSES):
+            nc.tensor.matmul_mx(
+                out=unread[:],
+                lhsT=zero_codes[:, 0:P].bitcast(FP8X4),
+                lhsT_scale=zero_scales[:, 0:P],
+                rhs=zero_codes[:].bitcast(FP8X4),
+                rhs_scale=zero_scales[:],
+                start=True,
+                stop=True,
+            )
 
         w_codes = const.tile([P, PASSES, N], U32, align_bytes=64)
         w_scales = const.tile([P, PASSES, N], U8, align_bytes=64)
@@ -98,7 +118,7 @@ def tile_binary_dense_s_kernel(tc, x, w, gamma, out):
                 grouped = resident.tile([P, PASSES * P * PACK], BF16, name="grouped", align_bytes=64)
                 dst = grouped[:].bitcast(F32).rearrange("p (g m u) -> p g m u", g=PASSES, u=HALVES)
                 src = xt[:].rearrange("p (g u) m -> p g m u", u=HALVES)
-                if j % VECTOR_EVERY == VECTOR_EVERY - 1:
+                if j % VECTOR_EVERY == 1:
                     nc.vector.tensor_copy(out=dst, in_=src)
                 else:
                     nc.scalar.copy(out=dst, in_=src)

@@ -7,7 +7,6 @@ BF16 = mybir.dt.bfloat16
 F32 = mybir.dt.float32
 U32 = mybir.dt.uint32
 U8 = mybir.dt.uint8
-I32 = mybir.dt.int32
 FP8X4 = mybir.dt.float8_e4m3fn_x4
 ACT = mybir.ActivationFunctionType
 ALU = mybir.AluOpType
@@ -24,11 +23,10 @@ HALVES = PACK // PAIR
 M_TILES = M // P
 ROUND = 2
 ROUNDS = M_TILES // ROUND
-LAG = 1
-W_ROUND = 0
-VECTOR_EVERY = 3
-WARM_PASSES = 8
-N_WARM = 512
+LAG = ROUNDS
+W_ROUND = 2
+N_SPREAD = 32
+VECTOR_EVERY = 4
 
 
 def tile_binary_dense_s_kernel(tc, x, w, gamma, out):
@@ -44,8 +42,11 @@ def tile_binary_dense_s_kernel(tc, x, w, gamma, out):
         x_view = x.rearrange("(p j) k -> p j k", j=M_TILES)
         out_view = out.rearrange("(p j) n -> p j n", j=M_TILES)
 
-        gamma_bf = const.tile([P, 1], BF16)
-        nc.scalar.dma_start(out=gamma_bf[:], in_=gamma.partition_broadcast(P))
+        gamma_row = const.tile([P, N_SPREAD], BF16)
+        nc.vector.memset(gamma_row[:], 0.0)
+        ones = const.tile([P, P], BF16)
+        nc.vector.memset(ones[:], 1.0)
+        nc.scalar.dma_start(out=gamma_row[0:1, 0:1], in_=gamma.unsqueeze(0))
 
         w_raw = const.tile([P, PASSES, PACK, N], BF16)
         x_rows = []
@@ -62,29 +63,14 @@ def tile_binary_dense_s_kernel(tc, x, w, gamma, out):
         ident = const.tile([P, P], F32)
         make_identity(nc, ident[:])
 
-        zeros = const.tile([P, N_WARM * PACK], BF16, align_bytes=64)
-        zero_codes = const.tile([P, N_WARM], U32, align_bytes=64)
-        zero_scales = const.tile([P, N_WARM], U8, align_bytes=64)
-        nc.vector.memset(zeros[:].bitcast(I32), 0)
-        nc.vector.quantize_mx(out=zero_codes[:].bitcast(FP8X4), scales=zero_scales[:], in_=zeros[:])
-        unread = flipped.tile([P, N_WARM], F32, name="xt")
-        for i in range(WARM_PASSES):
-            nc.tensor.matmul_mx(
-                out=unread[:],
-                lhsT=zero_codes[:, 0:P].bitcast(FP8X4),
-                lhsT_scale=zero_scales[:, 0:P],
-                rhs=zero_codes[:].bitcast(FP8X4),
-                rhs_scale=zero_scales[:],
-                start=True,
-                stop=True,
-            )
-
         w_codes = const.tile([P, PASSES, N], U32, align_bytes=64)
         w_scales = const.tile([P, PASSES, N], U8, align_bytes=64)
 
         def prepare_weights():
+            gamma_all = sums.tile([P, N_SPREAD], F32, name="acc")
+            nc.tensor.matmul(out=gamma_all[:], lhsT=ones[:], rhs=gamma_row[:], start=True, stop=True)
             gamma_abs = const.tile([P, 1], F32)
-            nc.scalar.activation(out=gamma_abs[:], in_=gamma_bf[:], func=ACT.Abs)
+            nc.scalar.activation(out=gamma_abs[:], in_=gamma_all[:, 0:1], func=ACT.Abs)
             w_sign = const.tile([P, PASSES, N, PACK], BF16)
             nc.scalar.activation(
                 out=w_sign[:],
@@ -118,7 +104,7 @@ def tile_binary_dense_s_kernel(tc, x, w, gamma, out):
                 grouped = resident.tile([P, PASSES * P * PACK], BF16, name="grouped", align_bytes=64)
                 dst = grouped[:].bitcast(F32).rearrange("p (g m u) -> p g m u", g=PASSES, u=HALVES)
                 src = xt[:].rearrange("p (g u) m -> p g m u", u=HALVES)
-                if j % VECTOR_EVERY == 1:
+                if j % VECTOR_EVERY == VECTOR_EVERY - 1:
                     nc.vector.tensor_copy(out=dst, in_=src)
                 else:
                     nc.scalar.copy(out=dst, in_=src)

@@ -21,12 +21,8 @@ PASSES = K // K_PASS
 PAIR = 2
 HALVES = PACK // PAIR
 M_TILES = M // P
-ROUND = 2
-ROUNDS = M_TILES // ROUND
-LAG = ROUNDS
-W_ROUND = 2
+LAST = M_TILES - 1
 N_SPREAD = 32
-VECTOR_EVERY = 4
 
 
 def tile_binary_dense_s_kernel(tc, x, w, gamma, out):
@@ -35,9 +31,9 @@ def tile_binary_dense_s_kernel(tc, x, w, gamma, out):
         ctx.enter_context(tc.manual_schedule())
         const = ctx.enter_context(tc.tile_pool(name="const", bufs=1))
         resident = ctx.enter_context(tc.tile_pool(name="resident", bufs=M_TILES))
-        results = ctx.enter_context(tc.tile_pool(name="results", bufs=ROUNDS))
-        flipped = ctx.enter_context(tc.psum_pool(name="flipped", bufs=2 * ROUND))
-        sums = ctx.enter_context(tc.psum_pool(name="sums", bufs=ROUNDS))
+        results = ctx.enter_context(tc.tile_pool(name="results", bufs=M_TILES))
+        flipped = ctx.enter_context(tc.psum_pool(name="flipped", bufs=4))
+        sums = ctx.enter_context(tc.psum_pool(name="sums", bufs=4))
 
         x_view = x.rearrange("(p j) k -> p j k", j=M_TILES)
         out_view = out.rearrange("(p j) n -> p j n", j=M_TILES)
@@ -46,16 +42,16 @@ def tile_binary_dense_s_kernel(tc, x, w, gamma, out):
         nc.vector.memset(gamma_row[:], 0.0)
         ones = const.tile([P, P], BF16)
         nc.vector.memset(ones[:], 1.0)
-        nc.scalar.dma_start(out=gamma_row[0:1, 0:1], in_=gamma.unsqueeze(0))
 
         w_raw = const.tile([P, PASSES, PACK, N], BF16)
         x_rows = []
         for j in range(M_TILES):
-            if j == ROUND * W_ROUND:
+            if j == 1:
                 nc.sync.dma_start(
                     out=w_raw[:].rearrange("p g (u e) n -> p (g u) e n", e=PAIR),
                     in_=w.rearrange("(c p e) n -> p c e n", c=PASSES * HALVES, e=PAIR),
                 )
+                nc.sync.dma_start(out=gamma_row[0:1, 0:1], in_=gamma.unsqueeze(0))
             x_tile = resident.tile([P, K], BF16, name="x_tile")
             nc.sync.dma_start(out=x_tile[:], in_=x_view[:, j, :])
             x_rows.append(x_tile)
@@ -65,19 +61,23 @@ def tile_binary_dense_s_kernel(tc, x, w, gamma, out):
 
         w_codes = const.tile([P, PASSES, N], U32, align_bytes=64)
         w_scales = const.tile([P, PASSES, N], U8, align_bytes=64)
+        gamma_abs = const.tile([P, 1], F32)
+        w_sign = const.tile([P, PASSES, N, PACK], BF16)
+        wb = const.tile([P, PASSES * N * PACK], BF16, align_bytes=64)
 
-        def prepare_weights():
+        def spread_gamma():
             gamma_all = sums.tile([P, N_SPREAD], F32, name="acc")
             nc.tensor.matmul(out=gamma_all[:], lhsT=ones[:], rhs=gamma_row[:], start=True, stop=True)
-            gamma_abs = const.tile([P, 1], F32)
             nc.scalar.activation(out=gamma_abs[:], in_=gamma_all[:, 0:1], func=ACT.Abs)
-            w_sign = const.tile([P, PASSES, N, PACK], BF16)
+
+        def sign_w():
             nc.scalar.activation(
                 out=w_sign[:],
                 in_=w_raw[:].rearrange("p g t n -> p g n t"),
                 func=ACT.Sign,
             )
-            wb = const.tile([P, PASSES * N * PACK], BF16, align_bytes=64)
+
+        def scale_w():
             nc.vector.tensor_scalar(
                 out=wb[:],
                 in0=w_sign[:].rearrange("p g n t -> p (g n t)"),
@@ -85,45 +85,54 @@ def tile_binary_dense_s_kernel(tc, x, w, gamma, out):
                 scalar2=None,
                 op0=ALU.mult,
             )
+
+        def quantise_w():
             nc.vector.quantize_mx(
                 out=w_codes[:].rearrange("p g n -> p (g n)").bitcast(FP8X4),
                 scales=w_scales[:].rearrange("p g n -> p (g n)"),
                 in_=wb[:],
             )
 
-        x_codes = []
-        x_scales = []
+        grouped_tiles = {}
+        x_codes = {}
+        x_scales = {}
 
-        def transpose_round(r):
-            grouped_tiles = []
-            for j in range(ROUND * r, ROUND * (r + 1)):
-                words = x_rows[j][:].bitcast(F32)
-                xt = flipped.tile([P, PASSES * HALVES, P], F32, name="xt")
-                for c in range(PASSES * HALVES):
-                    nc.tensor.transpose(xt[:, c, :], words[:, P * c : P * (c + 1)], ident[:])
-                grouped = resident.tile([P, PASSES * P * PACK], BF16, name="grouped", align_bytes=64)
-                dst = grouped[:].bitcast(F32).rearrange("p (g m u) -> p g m u", g=PASSES, u=HALVES)
-                src = xt[:].rearrange("p (g u) m -> p g m u", u=HALVES)
-                if j % VECTOR_EVERY == VECTOR_EVERY - 1:
-                    nc.vector.tensor_copy(out=dst, in_=src)
-                else:
-                    nc.scalar.copy(out=dst, in_=src)
-                grouped_tiles.append(grouped)
-            for grouped in grouped_tiles:
-                codes = resident.tile([P, PASSES, P], U32, name="codes", align_bytes=64)
-                scales = resident.tile([P, PASSES, P], U8, name="scales", align_bytes=64)
-                nc.vector.quantize_mx(
-                    out=codes[:].rearrange("p g m -> p (g m)").bitcast(FP8X4),
-                    scales=scales[:].rearrange("p g m -> p (g m)"),
-                    in_=grouped[:],
-                )
-                x_codes.append(codes)
-                x_scales.append(scales)
+        def flip(j, passes, engines):
+            if j not in grouped_tiles:
+                grouped_tiles[j] = resident.tile([P, PASSES, P * PACK], BF16, name="grouped", align_bytes=64)
+            grouped = grouped_tiles[j]
+            words = x_rows[j][:].bitcast(F32)
+            n = len(passes)
+            xt = flipped.tile([P, n, HALVES, P], F32, name="xt")
+            for i in range(n):
+                for u in range(HALVES):
+                    c = HALVES * passes[i] + u
+                    nc.tensor.transpose(xt[:, i, u, :], words[:, P * c : P * (c + 1)], ident[:])
+            flat = grouped[:].rearrange("p g f -> p (g f)")
+            dst = flat[:, P * PACK * passes[0] : P * PACK * (passes[0] + n)].bitcast(F32)
+            dst = dst.rearrange("p (g m u) -> p g m u", g=n, u=HALVES)
+            src = xt[:].rearrange("p g u m -> p g m u")
+            if engines == "V":
+                nc.vector.tensor_copy(out=dst, in_=src)
+            else:
+                nc.scalar.copy(out=dst, in_=src)
 
-        def multiply_round(r):
-            acc = sums.tile([P, ROUND, N], F32, name="acc")
-            for i in range(ROUND):
-                j = ROUND * r + i
+        def quantise(j, g0, g1):
+            if j not in x_codes:
+                x_codes[j] = resident.tile([P, PASSES, P], U32, name="codes", align_bytes=64)
+                x_scales[j] = resident.tile([P, PASSES, P], U8, name="scales", align_bytes=64)
+            codes = x_codes[j][:].rearrange("p g m -> p (g m)")
+            scales = x_scales[j][:].rearrange("p g m -> p (g m)")
+            nc.vector.quantize_mx(
+                out=codes[:, P * g0 : P * g1].bitcast(FP8X4),
+                scales=scales[:, P * g0 : P * g1],
+                in_=grouped_tiles[j][:].rearrange("p g f -> p (g f)")[:, P * PACK * g0 : P * PACK * g1],
+            )
+
+        def multiply(tiles):
+            acc = sums.tile([P, len(tiles), N], F32, name="acc")
+            for i in range(len(tiles)):
+                j = tiles[i]
                 for g in range(PASSES):
                     nc.tensor.matmul_mx(
                         out=acc[:, i, :],
@@ -134,14 +143,40 @@ def tile_binary_dense_s_kernel(tc, x, w, gamma, out):
                         start=(g == 0),
                         stop=(g == PASSES - 1),
                     )
-            result = results.tile([P, ROUND, N], F32, name="result")
-            nc.scalar.copy(out=result[:], in_=acc[:])
-            nc.sync.dma_start(out=out_view[:, ROUND * r : ROUND * (r + 1), :], in_=result[:])
+            return acc
 
-        for r in range(ROUNDS + LAG):
-            if r == W_ROUND:
-                prepare_weights()
-            if r < ROUNDS:
-                transpose_round(r)
-            if r >= LAG:
-                multiply_round(r - LAG)
+        def finish(tiles, acc, engine):
+            result = results.tile([P, len(tiles), N], F32, name="result")
+            if engine == "V":
+                nc.vector.tensor_copy(out=result[:], in_=acc[:])
+            else:
+                nc.scalar.copy(out=result[:], in_=acc[:])
+            nc.sync.dma_start(out=out_view[:, tiles[0] : tiles[0] + len(tiles), :], in_=result[:])
+
+        flip(0, [0, 1], "V")
+        quantise(0, 0, PASSES)
+        sign_w()
+        spread_gamma()
+        scale_w()
+        flip(1, [0, 1], "S")
+        quantise(1, 0, PASSES)
+        flip(2, [0, 1], "S")
+        flip(3, [0, 1], "V")
+        quantise_w()
+        quantise(2, 0, PASSES)
+        quantise(3, 0, PASSES)
+        flip(4, [0, 1], "S")
+        quantise(4, 0, PASSES)
+        flip(5, [0, 1], "S")
+        quantise(5, 0, PASSES)
+        flip(6, [0, 1], "S")
+        flip(LAST, [0], "V")
+        flip(LAST, [1], "S")
+        quantise(6, 0, PASSES)
+        quantise(LAST, 0, 1)
+        quantise(LAST, 1, 2)
+        finish([0, 1], multiply([0, 1]), "S")
+        finish([2, 3], multiply([2, 3]), "S")
+        finish([4, 5], multiply([4, 5]), "V")
+        finish([6], multiply([6]), "S")
+        finish([7], multiply([7]), "S")

@@ -22,6 +22,7 @@ PAIR = 2
 HALVES = PACK // PAIR
 M_TILES = M // P
 LAST = M_TILES - 1
+WAKE_MATMULS = 4
 N_SPREAD = 32
 
 
@@ -38,6 +39,8 @@ def tile_binary_dense_s_kernel(tc, x, w, gamma, out):
         x_view = x.rearrange("(p j) k -> p j k", j=M_TILES)
         out_view = out.rearrange("(p j) n -> p j n", j=M_TILES)
 
+        warm_in = const.tile([P, P], F32)
+        nc.vector.memset(warm_in[:], 1.0)
         gamma_row = const.tile([P, N_SPREAD], BF16)
         nc.vector.memset(gamma_row[:], 0.0)
         ones = const.tile([P, P], BF16)
@@ -94,6 +97,11 @@ def tile_binary_dense_s_kernel(tc, x, w, gamma, out):
             )
 
         grouped_tiles = {}
+        def wake_tensor_engine():
+            for i in range(WAKE_MATMULS):
+                warm_out = flipped.tile([P, P], F32, name="xt")
+                nc.tensor.matmul(out=warm_out[:], lhsT=warm_in[:], rhs=warm_in[:], start=True, stop=True)
+
         x_codes = {}
         x_scales = {}
 
@@ -153,16 +161,17 @@ def tile_binary_dense_s_kernel(tc, x, w, gamma, out):
                 nc.scalar.copy(out=result[:], in_=acc[:])
             nc.sync.dma_start(out=out_view[:, tiles[0] : tiles[0] + len(tiles), :], in_=result[:])
 
+        wake_tensor_engine()
         flip(0, [0, 1], "V")
-        quantise(0, 0, PASSES)
         sign_w()
         spread_gamma()
         scale_w()
+        quantise(0, 0, PASSES)
+        quantise_w()
         flip(1, [0, 1], "S")
         quantise(1, 0, PASSES)
         flip(2, [0, 1], "S")
         flip(3, [0, 1], "V")
-        quantise_w()
         quantise(2, 0, PASSES)
         quantise(3, 0, PASSES)
         flip(4, [0, 1], "S")

@@ -48,16 +48,17 @@ def tile_binary_dense_s_kernel(tc, x, w, gamma, out):
 
         w_raw = const.tile([P, PASSES, PACK, N], BF16)
         x_rows = []
-        for j in range(M_TILES):
-            if j == 1:
+        for first, count in ((0, 1), (1, 2), (3, 2), (5, 2), (7, 1)):
+            if first == 1:
                 nc.sync.dma_start(
                     out=w_raw[:].rearrange("p g (u e) n -> p (g u) e n", e=PAIR),
                     in_=w.rearrange("(c p e) n -> p c e n", c=PASSES * HALVES, e=PAIR),
                 )
                 nc.sync.dma_start(out=gamma_row[0:1, 0:1], in_=gamma.unsqueeze(0))
-            x_tile = resident.tile([P, K], BF16, name="x_tile")
-            nc.sync.dma_start(out=x_tile[:], in_=x_view[:, j, :])
-            x_rows.append(x_tile)
+            x_tile = const.tile([P, count, K], BF16, name="x_tile%d" % first)
+            nc.sync.dma_start(out=x_tile[:], in_=x_view[:, first : first + count, :])
+            for i in range(count):
+                x_rows.append(x_tile[:, i, :])
 
         ident = const.tile([P, P], F32)
         make_identity(nc, ident[:])
@@ -109,7 +110,7 @@ def tile_binary_dense_s_kernel(tc, x, w, gamma, out):
             if j not in grouped_tiles:
                 grouped_tiles[j] = resident.tile([P, PASSES, P * PACK], BF16, name="grouped", align_bytes=64)
             grouped = grouped_tiles[j]
-            words = x_rows[j][:].bitcast(F32)
+            words = x_rows[j].bitcast(F32)
             n = len(passes)
             xt = flipped.tile([P, n, HALVES, P], F32, name="xt")
             for i in range(n):

@@ -50,7 +50,7 @@ def tile_binary_dense_s_kernel(tc, x, w, gamma, out):
         x_rows = []
         for first, count in ((0, 1), (1, 2), (3, 2), (5, 2), (7, 1)):
             if first == 1:
-                nc.sync.dma_start(
+                nc.scalar.dma_start(
                     out=w_raw[:].rearrange("p g (u e) n -> p (g u) e n", e=PAIR),
                     in_=w.rearrange("(c p e) n -> p c e n", c=PASSES * HALVES, e=PAIR),
                 )

@@ -48,7 +48,7 @@ def tile_binary_dense_s_kernel(tc, x, w, gamma, out):
 
         w_raw = const.tile([P, PASSES, PACK, N], BF16)
         x_rows = []
-        for first, count in ((0, 1), (1, 2), (3, 2), (5, 2), (7, 1)):
+        for first, count in ((0, 1), (1, 2), (3, 2), (5, 1), (6, 1), (7, 1)):
             if first == 1:
                 nc.scalar.dma_start(
                     out=w_raw[:].rearrange("p g (u e) n -> p (g u) e n", e=PAIR),
@@ -56,7 +56,12 @@ def tile_binary_dense_s_kernel(tc, x, w, gamma, out):
                 )
                 nc.sync.dma_start(out=gamma_row[0:1, 0:1], in_=gamma.unsqueeze(0))
             x_tile = const.tile([P, count, K], BF16, name="x_tile%d" % first)
-            nc.sync.dma_start(out=x_tile[:], in_=x_view[:, first : first + count, :])
+            width = K_PASS if first == LAST else K
+            for k0 in range(0, K, width):
+                nc.sync.dma_start(
+                    out=x_tile[:, :, k0 : k0 + width],
+                    in_=x_view[:, first : first + count, k0 : k0 + width],
+                )
             for i in range(count):
                 x_rows.append(x_tile[:, i, :])
 
@@ -177,6 +182,7 @@ def tile_binary_dense_s_kernel(tc, x, w, gamma, out):
         quantise(3, 0, PASSES)
         flip(4, [0, 1], "S")
         quantise(4, 0, PASSES)
+        finish([0, 1], multiply([0, 1]), "S")
         flip(5, [0, 1], "S")
         quantise(5, 0, PASSES)
         flip(6, [0, 1], "S")
@@ -185,7 +191,6 @@ def tile_binary_dense_s_kernel(tc, x, w, gamma, out):
         quantise(6, 0, PASSES)
         quantise(LAST, 0, 1)
         quantise(LAST, 1, 2)
-        finish([0, 1], multiply([0, 1]), "S")
         finish([2, 3], multiply([2, 3]), "S")
         finish([4, 5], multiply([4, 5]), "V")
         finish([6], multiply([6]), "S")

@@ -22,7 +22,6 @@ PAIR = 2
 HALVES = PACK // PAIR
 M_TILES = M // P
 LAST = M_TILES - 1
-WAKE_MATMULS = 4
 N_SPREAD = 32
 
 
@@ -103,8 +102,8 @@ def tile_binary_dense_s_kernel(tc, x, w, gamma, out):
             )
 
         grouped_tiles = {}
-        def wake_tensor_engine():
-            for i in range(WAKE_MATMULS):
+        def wake_tensor_engine(matmuls):
+            for i in range(matmuls):
                 warm_out = flipped.tile([P, P], F32, name="xt")
                 nc.tensor.matmul(out=warm_out[:], lhsT=warm_in[:], rhs=warm_in[:], start=True, stop=True)
 
@@ -167,16 +166,18 @@ def tile_binary_dense_s_kernel(tc, x, w, gamma, out):
                 nc.scalar.copy(out=result[:], in_=acc[:])
             nc.sync.dma_start(out=out_view[:, tiles[0] : tiles[0] + len(tiles), :], in_=result[:])
 
-        wake_tensor_engine()
+        wake_tensor_engine(3)
         flip(0, [0, 1], "V")
         sign_w()
         spread_gamma()
         scale_w()
         quantise(0, 0, PASSES)
         quantise_w()
+        wake_tensor_engine(2)
         flip(1, [0, 1], "S")
         quantise(1, 0, PASSES)
         flip(2, [0, 1], "S")
+        wake_tensor_engine(1)
         flip(3, [0, 1], "V")
         quantise(2, 0, PASSES)
         quantise(3, 0, PASSES)

@@ -47,7 +47,7 @@ def tile_binary_dense_s_kernel(tc, x, w, gamma, out):
 
         w_raw = const.tile([P, PASSES, PACK, N], BF16)
         x_rows = []
-        for first, count in ((0, 1), (1, 2), (3, 2), (5, 1), (6, 1), (7, 1)):
+        for first, count in ((0, 1), (1, 1), (2, 1), (3, 1), (4, 1), (5, 1), (6, 1), (7, 1)):
             if first == 1:
                 nc.scalar.dma_start(
                     out=w_raw[:].rearrange("p g (u e) n -> p (g u) e n", e=PAIR),
@@ -173,7 +173,7 @@ def tile_binary_dense_s_kernel(tc, x, w, gamma, out):
         scale_w()
         quantise(0, 0, PASSES)
         quantise_w()
-        wake_tensor_engine(2)
+        wake_tensor_engine(1)
         flip(1, [0, 1], "S")
         quantise(1, 0, PASSES)
         flip(2, [0, 1], "S")
@@ -183,8 +183,9 @@ def tile_binary_dense_s_kernel(tc, x, w, gamma, out):
         quantise(3, 0, PASSES)
         flip(4, [0, 1], "S")
         quantise(4, 0, PASSES)
-        finish([0, 1], multiply([0, 1]), "S")
+        wake_tensor_engine(1)
         flip(5, [0, 1], "S")
+        finish([0, 1], multiply([0, 1]), "V")
         quantise(5, 0, PASSES)
         flip(6, [0, 1], "S")
         flip(LAST, [0], "V")
@@ -193,6 +194,6 @@ def tile_binary_dense_s_kernel(tc, x, w, gamma, out):
         quantise(LAST, 0, 1)
         quantise(LAST, 1, 2)
         finish([2, 3], multiply([2, 3]), "S")
-        finish([4, 5], multiply([4, 5]), "V")
-        finish([6], multiply([6]), "S")
+        finish([4, 5], multiply([4, 5]), "S")
+        finish([6], multiply([6]), "V")
         finish([7], multiply([7]), "S")

@@ -32,8 +32,8 @@ def tile_binary_dense_s_kernel(tc, x, w, gamma, out):
         const = ctx.enter_context(tc.tile_pool(name="const", bufs=1))
         resident = ctx.enter_context(tc.tile_pool(name="resident", bufs=M_TILES))
         results = ctx.enter_context(tc.tile_pool(name="results", bufs=M_TILES))
-        flipped = ctx.enter_context(tc.psum_pool(name="flipped", bufs=4))
-        sums = ctx.enter_context(tc.psum_pool(name="sums", bufs=4))
+        flipped = ctx.enter_context(tc.psum_pool(name="flipped", bufs=5))
+        sums = ctx.enter_context(tc.psum_pool(name="sums", bufs=3))
 
         x_view = x.rearrange("(p j) k -> p j k", j=M_TILES)
         out_view = out.rearrange("(p j) n -> p j n", j=M_TILES)
@@ -173,7 +173,7 @@ def tile_binary_dense_s_kernel(tc, x, w, gamma, out):
         scale_w()
         quantise(0, 0, PASSES)
         quantise_w()
-        wake_tensor_engine(1)
+        wake_tensor_engine(2)
         flip(1, [0, 1], "S")
         quantise(1, 0, PASSES)
         flip(2, [0, 1], "S")
@@ -183,9 +183,8 @@ def tile_binary_dense_s_kernel(tc, x, w, gamma, out):
         quantise(3, 0, PASSES)
         flip(4, [0, 1], "S")
         quantise(4, 0, PASSES)
-        wake_tensor_engine(1)
-        flip(5, [0, 1], "S")
         finish([0, 1], multiply([0, 1]), "V")
+        flip(5, [0, 1], "S")
         quantise(5, 0, PASSES)
         flip(6, [0, 1], "S")
         flip(LAST, [0], "V")

@@ -38,8 +38,6 @@ def tile_binary_dense_s_kernel(tc, x, w, gamma, out):
         x_view = x.rearrange("(p j) k -> p j k", j=M_TILES)
         out_view = out.rearrange("(p j) n -> p j n", j=M_TILES)
 
-        warm_in = const.tile([P, P], F32)
-        nc.vector.memset(warm_in[:], 1.0)
         gamma_row = const.tile([P, N_SPREAD], BF16)
         nc.vector.memset(gamma_row[:], 0.0)
         ones = const.tile([P, P], BF16)
@@ -105,7 +103,7 @@ def tile_binary_dense_s_kernel(tc, x, w, gamma, out):
         def wake_tensor_engine(matmuls):
             for i in range(matmuls):
                 warm_out = flipped.tile([P, P], F32, name="xt")
-                nc.tensor.matmul(out=warm_out[:], lhsT=warm_in[:], rhs=warm_in[:], start=True, stop=True)
+                nc.tensor.matmul(out=warm_out[:], lhsT=ident[:], rhs=ident[:], start=True, stop=True)
 
         x_codes = {}
         x_scales = {}
@@ -173,9 +171,10 @@ def tile_binary_dense_s_kernel(tc, x, w, gamma, out):
         scale_w()
         quantise(0, 0, PASSES)
         quantise_w()
-        wake_tensor_engine(2)
+        wake_tensor_engine(1)
         flip(1, [0, 1], "S")
         quantise(1, 0, PASSES)
+        wake_tensor_engine(1)
         flip(2, [0, 1], "S")
         wake_tensor_engine(1)
         flip(3, [0, 1], "V")

@@ -44,14 +44,13 @@ def tile_binary_dense_s_kernel(tc, x, w, gamma, out):
         nc.vector.memset(ones[:], 1.0)
 
         w_raw = const.tile([P, PASSES, PACK, N], BF16)
+        nc.sync.dma_start(
+            out=w_raw[:].rearrange("p g (u e) n -> p (g u) e n", e=PAIR),
+            in_=w.rearrange("(c p e) n -> p c e n", c=PASSES * HALVES, e=PAIR),
+        )
+        nc.sync.dma_start(out=gamma_row[0:1, 0:1], in_=gamma.unsqueeze(0))
         x_rows = []
         for first, count in ((0, 1), (1, 1), (2, 1), (3, 1), (4, 1), (5, 1), (6, 1), (7, 1)):
-            if first == 1:
-                nc.scalar.dma_start(
-                    out=w_raw[:].rearrange("p g (u e) n -> p (g u) e n", e=PAIR),
-                    in_=w.rearrange("(c p e) n -> p c e n", c=PASSES * HALVES, e=PAIR),
-                )
-                nc.sync.dma_start(out=gamma_row[0:1, 0:1], in_=gamma.unsqueeze(0))
             x_tile = const.tile([P, count, K], BF16, name="x_tile%d" % first)
             width = K_PASS if first == LAST else K
             for k0 in range(0, K, width):
@@ -140,8 +139,8 @@ def tile_binary_dense_s_kernel(tc, x, w, gamma, out):
                 in_=grouped_tiles[j][:].rearrange("p g f -> p (g f)")[:, P * PACK * g0 : P * PACK * g1],
             )
 
-        def multiply(tiles):
-            acc = sums.tile([P, len(tiles), N], F32, name="acc")
+        def multiply(tiles, pool=sums, tag="acc"):
+            acc = pool.tile([P, len(tiles), N], F32, name=tag)
             for i in range(len(tiles)):
                 j = tiles[i]
                 for g in range(PASSES):
@@ -164,34 +163,35 @@ def tile_binary_dense_s_kernel(tc, x, w, gamma, out):
                 nc.scalar.copy(out=result[:], in_=acc[:])
             nc.sync.dma_start(out=out_view[:, tiles[0] : tiles[0] + len(tiles), :], in_=result[:])
 
-        wake_tensor_engine(3)
-        flip(0, [0, 1], "V")
+        wake_tensor_engine(4)
         sign_w()
         spread_gamma()
         scale_w()
-        quantise(0, 0, PASSES)
+        flip(0, [0, 1], "S")
         quantise_w()
         wake_tensor_engine(1)
         flip(1, [0, 1], "S")
+        quantise(0, 0, PASSES)
+        flip(2, [0, 1], "S")
         quantise(1, 0, PASSES)
         wake_tensor_engine(1)
-        flip(2, [0, 1], "S")
-        wake_tensor_engine(1)
-        flip(3, [0, 1], "V")
+        flip(3, [0, 1], "S")
         quantise(2, 0, PASSES)
-        quantise(3, 0, PASSES)
         flip(4, [0, 1], "S")
-        quantise(4, 0, PASSES)
+        quantise(3, 0, PASSES)
         finish([0, 1], multiply([0, 1]), "V")
-        flip(5, [0, 1], "S")
-        quantise(5, 0, PASSES)
-        flip(6, [0, 1], "S")
-        flip(LAST, [0], "V")
+        quantise(4, 0, PASSES)
+        flip(5, [0], "S")
+        flip(5, [1], "S")
+        flip(6, [0], "V")
+        flip(6, [1], "S")
+        flip(LAST, [0], "S")
         flip(LAST, [1], "S")
+        quantise(5, 0, PASSES)
         quantise(6, 0, PASSES)
         quantise(LAST, 0, 1)
         quantise(LAST, 1, 2)
         finish([2, 3], multiply([2, 3]), "S")
-        finish([4, 5], multiply([4, 5]), "S")
-        finish([6], multiply([6]), "V")
-        finish([7], multiply([7]), "S")
+        finish([4, 5], multiply([4, 5]), "V")
+        finish([6], multiply([6]), "S")
+        finish([7], multiply([7], pool=flipped, tag="xt"), "V")

@@ -22,6 +22,7 @@ PAIR = 2
 HALVES = PACK // PAIR
 M_TILES = M // P
 LAST = M_TILES - 1
+N_IDLE = 512
 N_SPREAD = 32
 
 
@@ -40,8 +41,11 @@ def tile_binary_dense_s_kernel(tc, x, w, gamma, out):
 
         gamma_row = const.tile([P, N_SPREAD], BF16)
         nc.vector.memset(gamma_row[:], 0.0)
-        ones = const.tile([P, P], BF16)
+        ones = const.tile([P, PACK * N_IDLE], BF16, align_bytes=64)
         nc.vector.memset(ones[:], 1.0)
+        idle_codes = const.tile([P, N_IDLE], U32, align_bytes=64)
+        idle_scales = const.tile([P, N_IDLE], U8, align_bytes=64)
+        nc.vector.quantize_mx(out=idle_codes[:].bitcast(FP8X4), scales=idle_scales[:], in_=ones[:])
 
         w_raw = const.tile([P, PASSES, PACK, N], BF16)
         nc.sync.dma_start(
@@ -72,7 +76,7 @@ def tile_binary_dense_s_kernel(tc, x, w, gamma, out):
 
         def spread_gamma():
             gamma_all = sums.tile([P, N_SPREAD], F32, name="acc")
-            nc.tensor.matmul(out=gamma_all[:], lhsT=ones[:], rhs=gamma_row[:], start=True, stop=True)
+            nc.tensor.matmul(out=gamma_all[:], lhsT=ones[:, :P], rhs=gamma_row[:], start=True, stop=True)
             nc.scalar.activation(out=gamma_abs[:], in_=gamma_all[:, 0:1], func=ACT.Abs)
 
         def sign_w():
@@ -99,6 +103,19 @@ def tile_binary_dense_s_kernel(tc, x, w, gamma, out):
             )
 
         grouped_tiles = {}
+        def idle_passes(passes):
+            for i in range(passes):
+                idle_out = flipped.tile([P, N_IDLE], F32, name="xt")
+                nc.tensor.matmul_mx(
+                    out=idle_out[:],
+                    lhsT=idle_codes[:, :P].bitcast(FP8X4),
+                    lhsT_scale=idle_scales[:, :P],
+                    rhs=idle_codes[:].bitcast(FP8X4),
+                    rhs_scale=idle_scales[:],
+                    start=True,
+                    stop=True,
+                )
+
         def wake_tensor_engine(matmuls):
             for i in range(matmuls):
                 warm_out = flipped.tile([P, P], F32, name="xt")
@@ -163,7 +180,7 @@ def tile_binary_dense_s_kernel(tc, x, w, gamma, out):
                 nc.scalar.copy(out=result[:], in_=acc[:])
             nc.sync.dma_start(out=out_view[:, tiles[0] : tiles[0] + len(tiles), :], in_=result[:])
 
-        wake_tensor_engine(4)
+        idle_passes(3)
         sign_w()
         spread_gamma()
         scale_w()
@@ -172,11 +189,13 @@ def tile_binary_dense_s_kernel(tc, x, w, gamma, out):
         wake_tensor_engine(1)
         flip(1, [0, 1], "S")
         quantise(0, 0, PASSES)
+        wake_tensor_engine(1)
         flip(2, [0, 1], "S")
         quantise(1, 0, PASSES)
         wake_tensor_engine(1)
         flip(3, [0, 1], "S")
         quantise(2, 0, PASSES)
+        wake_tensor_engine(1)
         flip(4, [0, 1], "S")
         quantise(3, 0, PASSES)
         finish([0, 1], multiply([0, 1]), "V")

@@ -22,7 +22,7 @@ PAIR = 2
 HALVES = PACK // PAIR
 M_TILES = M // P
 LAST = M_TILES - 1
-N_IDLE = 512
+N_IDLE = 256
 N_SPREAD = 32
 
 
@@ -41,11 +41,13 @@ def tile_binary_dense_s_kernel(tc, x, w, gamma, out):
 
         gamma_row = const.tile([P, N_SPREAD], BF16)
         nc.vector.memset(gamma_row[:], 0.0)
-        ones = const.tile([P, PACK * N_IDLE], BF16, align_bytes=64)
+        ones = const.tile([P, P], BF16)
         nc.vector.memset(ones[:], 1.0)
+        zeros = const.tile([P, PACK * N_IDLE], BF16, align_bytes=64)
+        nc.vector.memset(zeros[:].bitcast(U32), 0)
         idle_codes = const.tile([P, N_IDLE], U32, align_bytes=64)
         idle_scales = const.tile([P, N_IDLE], U8, align_bytes=64)
-        nc.vector.quantize_mx(out=idle_codes[:].bitcast(FP8X4), scales=idle_scales[:], in_=ones[:])
+        nc.vector.quantize_mx(out=idle_codes[:].bitcast(FP8X4), scales=idle_scales[:], in_=zeros[:])
 
         w_raw = const.tile([P, PASSES, PACK, N], BF16)
         nc.sync.dma_start(
@@ -76,7 +78,7 @@ def tile_binary_dense_s_kernel(tc, x, w, gamma, out):
 
         def spread_gamma():
             gamma_all = sums.tile([P, N_SPREAD], F32, name="acc")
-            nc.tensor.matmul(out=gamma_all[:], lhsT=ones[:, :P], rhs=gamma_row[:], start=True, stop=True)
+            nc.tensor.matmul(out=gamma_all[:], lhsT=ones[:], rhs=gamma_row[:], start=True, stop=True)
             nc.scalar.activation(out=gamma_abs[:], in_=gamma_all[:, 0:1], func=ACT.Abs)
 
         def sign_w():
@@ -180,7 +182,7 @@ def tile_binary_dense_s_kernel(tc, x, w, gamma, out):
                 nc.scalar.copy(out=result[:], in_=acc[:])
             nc.sync.dma_start(out=out_view[:, tiles[0] : tiles[0] + len(tiles), :], in_=result[:])
 
-        idle_passes(3)
+        idle_passes(6)
         sign_w()
         spread_gamma()
         scale_w()

from contextlib import ExitStack

import concourse.mybir as mybir
from concourse.masks import make_identity

BF16 = mybir.dt.bfloat16
F32 = mybir.dt.float32
U32 = mybir.dt.uint32
U8 = mybir.dt.uint8
FP8X4 = mybir.dt.float8_e4m3fn_x4
ACT = mybir.ActivationFunctionType
ALU = mybir.AluOpType

M, K, N = 1024, 1024, 128
FLOPS = 2 * M * K * N

P = 128
PACK = 4
K_PASS = P * PACK
PASSES = K // K_PASS
PAIR = 2
HALVES = PACK // PAIR
M_TILES = M // P
LAST = M_TILES - 1
N_IDLE = 256
N_SPREAD = 32


def tile_binary_dense_s_kernel(tc, x, w, gamma, out):
    nc = tc.nc
    with ExitStack() as ctx:
        ctx.enter_context(tc.manual_schedule())
        const = ctx.enter_context(tc.tile_pool(name="const", bufs=1))
        resident = ctx.enter_context(tc.tile_pool(name="resident", bufs=M_TILES))
        results = ctx.enter_context(tc.tile_pool(name="results", bufs=M_TILES))
        flipped = ctx.enter_context(tc.psum_pool(name="flipped", bufs=5))
        sums = ctx.enter_context(tc.psum_pool(name="sums", bufs=3))

        x_view = x.rearrange("(p j) k -> p j k", j=M_TILES)
        out_view = out.rearrange("(p j) n -> p j n", j=M_TILES)

        gamma_row = const.tile([P, N_SPREAD], BF16)
        nc.vector.memset(gamma_row[:], 0.0)
        ones = const.tile([P, P], BF16)
        nc.vector.memset(ones[:], 1.0)
        zeros = const.tile([P, PACK * N_IDLE], BF16, align_bytes=64)
        nc.vector.memset(zeros[:].bitcast(U32), 0)
        idle_codes = const.tile([P, N_IDLE], U32, align_bytes=64)
        idle_scales = const.tile([P, N_IDLE], U8, align_bytes=64)
        nc.vector.quantize_mx(out=idle_codes[:].bitcast(FP8X4), scales=idle_scales[:], in_=zeros[:])

        w_raw = const.tile([P, PASSES, PACK, N], BF16)
        nc.sync.dma_start(
            out=w_raw[:].rearrange("p g (u e) n -> p (g u) e n", e=PAIR),
            in_=w.rearrange("(c p e) n -> p c e n", c=PASSES * HALVES, e=PAIR),
        )
        nc.sync.dma_start(out=gamma_row[0:1, 0:1], in_=gamma.unsqueeze(0))
        x_rows = []
        for first, count in ((0, 1), (1, 1), (2, 1), (3, 1), (4, 1), (5, 1), (6, 1), (7, 1)):
            x_tile = const.tile([P, count, K], BF16, name="x_tile%d" % first)
            width = K_PASS if first == LAST else K
            for k0 in range(0, K, width):
                nc.sync.dma_start(
                    out=x_tile[:, :, k0 : k0 + width],
                    in_=x_view[:, first : first + count, k0 : k0 + width],
                )
            for i in range(count):
                x_rows.append(x_tile[:, i, :])

        ident = const.tile([P, P], F32)
        make_identity(nc, ident[:])

        w_codes = const.tile([P, PASSES, N], U32, align_bytes=64)
        w_scales = const.tile([P, PASSES, N], U8, align_bytes=64)
        gamma_abs = const.tile([P, 1], F32)
        w_sign = const.tile([P, PASSES, N, PACK], BF16)
        wb = const.tile([P, PASSES * N * PACK], BF16, align_bytes=64)

        def spread_gamma():
            gamma_all = sums.tile([P, N_SPREAD], F32, name="acc")
            nc.tensor.matmul(out=gamma_all[:], lhsT=ones[:], rhs=gamma_row[:], start=True, stop=True)
            nc.scalar.activation(out=gamma_abs[:], in_=gamma_all[:, 0:1], func=ACT.Abs)

        def sign_w():
            nc.scalar.activation(
                out=w_sign[:],
                in_=w_raw[:].rearrange("p g t n -> p g n t"),
                func=ACT.Sign,
            )

        def scale_w():
            nc.vector.tensor_scalar(
                out=wb[:],
                in0=w_sign[:].rearrange("p g n t -> p (g n t)"),
                scalar1=gamma_abs[:, 0:1],
                scalar2=None,
                op0=ALU.mult,
            )

        def quantise_w():
            nc.vector.quantize_mx(
                out=w_codes[:].rearrange("p g n -> p (g n)").bitcast(FP8X4),
                scales=w_scales[:].rearrange("p g n -> p (g n)"),
                in_=wb[:],
            )

        grouped_tiles = {}
        def idle_passes(passes):
            for i in range(passes):
                idle_out = flipped.tile([P, N_IDLE], F32, name="xt")
                nc.tensor.matmul_mx(
                    out=idle_out[:],
                    lhsT=idle_codes[:, :P].bitcast(FP8X4),
                    lhsT_scale=idle_scales[:, :P],
                    rhs=idle_codes[:].bitcast(FP8X4),
                    rhs_scale=idle_scales[:],
                    start=True,
                    stop=True,
                )

        def wake_tensor_engine(matmuls):
            for i in range(matmuls):
                warm_out = flipped.tile([P, P], F32, name="xt")
                nc.tensor.matmul(out=warm_out[:], lhsT=ident[:], rhs=ident[:], start=True, stop=True)

        x_codes = {}
        x_scales = {}

        def flip(j, passes, engines):
            if j not in grouped_tiles:
                grouped_tiles[j] = resident.tile([P, PASSES, P * PACK], BF16, name="grouped", align_bytes=64)
            grouped = grouped_tiles[j]
            words = x_rows[j].bitcast(F32)
            n = len(passes)
            xt = flipped.tile([P, n, HALVES, P], F32, name="xt")
            for i in range(n):
                for u in range(HALVES):
                    c = HALVES * passes[i] + u
                    nc.tensor.transpose(xt[:, i, u, :], words[:, P * c : P * (c + 1)], ident[:])
            flat = grouped[:].rearrange("p g f -> p (g f)")
            dst = flat[:, P * PACK * passes[0] : P * PACK * (passes[0] + n)].bitcast(F32)
            dst = dst.rearrange("p (g m u) -> p g m u", g=n, u=HALVES)
            src = xt[:].rearrange("p g u m -> p g m u")
            if engines == "V":
                nc.vector.tensor_copy(out=dst, in_=src)
            else:
                nc.scalar.copy(out=dst, in_=src)

        def quantise(j, g0, g1):
            if j not in x_codes:
                x_codes[j] = resident.tile([P, PASSES, P], U32, name="codes", align_bytes=64)
                x_scales[j] = resident.tile([P, PASSES, P], U8, name="scales", align_bytes=64)
            codes = x_codes[j][:].rearrange("p g m -> p (g m)")
            scales = x_scales[j][:].rearrange("p g m -> p (g m)")
            nc.vector.quantize_mx(
                out=codes[:, P * g0 : P * g1].bitcast(FP8X4),
                scales=scales[:, P * g0 : P * g1],
                in_=grouped_tiles[j][:].rearrange("p g f -> p (g f)")[:, P * PACK * g0 : P * PACK * g1],
            )

        def multiply(tiles, pool=sums, tag="acc"):
            acc = pool.tile([P, len(tiles), N], F32, name=tag)
            for i in range(len(tiles)):
                j = tiles[i]
                for g in range(PASSES):
                    nc.tensor.matmul_mx(
                        out=acc[:, i, :],
                        lhsT=x_codes[j][:, g, :].bitcast(FP8X4),
                        lhsT_scale=x_scales[j][:, g, :],
                        rhs=w_codes[:, g, :].bitcast(FP8X4),
                        rhs_scale=w_scales[:, g, :],
                        start=(g == 0),
                        stop=(g == PASSES - 1),
                    )
            return acc

        def finish(tiles, acc, engine):
            result = results.tile([P, len(tiles), N], F32, name="result")
            if engine == "V":
                nc.vector.tensor_copy(out=result[:], in_=acc[:])
            else:
                nc.scalar.copy(out=result[:], in_=acc[:])
            nc.sync.dma_start(out=out_view[:, tiles[0] : tiles[0] + len(tiles), :], in_=result[:])

        idle_passes(6)
        sign_w()
        spread_gamma()
        scale_w()
        flip(0, [0, 1], "S")
        quantise_w()
        wake_tensor_engine(1)
        flip(1, [0, 1], "S")
        quantise(0, 0, PASSES)
        wake_tensor_engine(1)
        flip(2, [0, 1], "S")
        quantise(1, 0, PASSES)
        wake_tensor_engine(1)
        flip(3, [0, 1], "S")
        quantise(2, 0, PASSES)
        wake_tensor_engine(1)
        flip(4, [0, 1], "S")
        quantise(3, 0, PASSES)
        finish([0, 1], multiply([0, 1]), "V")
        quantise(4, 0, PASSES)
        flip(5, [0], "S")
        flip(5, [1], "S")
        flip(6, [0], "V")
        flip(6, [1], "S")
        flip(LAST, [0], "S")
        flip(LAST, [1], "S")
        quantise(5, 0, PASSES)
        quantise(6, 0, PASSES)
        quantise(LAST, 0, 1)
        quantise(LAST, 1, 2)
        finish([2, 3], multiply([2, 3]), "S")
        finish([4, 5], multiply([4, 5]), "V")
        finish([6], multiply([6]), "S")
        finish([7], multiply([7], pool=flipped, tag="xt"), "V")
